import numpy as np
import ml_dtypes


def mxq(x, axis, fmt="e4m3"):
    dtype, down = {"e4m3": (ml_dtypes.float8_e4m3fn, 7), "e5m2": (ml_dtypes.float8_e5m2, 14)}[fmt]
    v = np.moveaxis(np.asarray(x, np.float32).astype(ml_dtypes.bfloat16).astype(np.float64), axis, -1)
    blocks = v.reshape(v.shape[:-1] + (-1, 32))
    amax = np.abs(blocks).max(-1, keepdims=True)
    byte = np.maximum(np.where(amax > 0, np.frexp(amax)[1] - 1 + 127, 0) - down, 1)
    scale = np.exp2(byte - 127.0)
    codes = (blocks / scale).astype(np.float32).astype(dtype).astype(np.float64)
    return np.moveaxis((codes * scale).reshape(v.shape), -1, axis)


WIDE = False


def mx_kscale(k):
    if not WIDE:
        return np.ones(k)
    levels = np.array([10, -10, 5, -5, 0])
    if k % 512:
        return np.exp2(np.random.permutation(np.resize(levels, k // 32))).repeat(32)
    a = np.empty((k // 512, 16))
    for p in range(k // 512):
        a[p, :8] = np.random.permutation(np.resize(levels, 8))
        for g in range(8):
            far = levels[np.abs(levels - a[p, g]) >= 10]
            a[p, g + 8] = far[np.random.randint(len(far))]
    return np.exp2(a.ravel()).repeat(32)


BF16 = ml_dtypes.bfloat16


def bf(x):
    return np.asarray(x, np.float32).astype(BF16)


def f64(x):
    return np.asarray(x).astype(np.float64)


N, N_CH, X, H = 4096, 4, 512, 256
K = N_CH * H


def sigmoid(v):
    return 1.0 / (1.0 + np.exp(-v))


def setup_inputs():
    s, t = mx_kscale(X), mx_kscale(K)
    return {
        "x": bf(np.random.standard_normal((N, X)) * s),
        "x_mask": bf(np.random.random(N) < 0.75),
        "neighbour_h": bf(np.random.standard_normal((N, N_CH, H)) * t.reshape(N_CH, H)),
        "neighbour_c": bf(np.random.standard_normal((N, N_CH, H))),
        "W_f_in": bf(np.random.standard_normal((X, H)) * 0.5 / np.sqrt(X) / s[:, None]),
        "b_f_in": bf(np.random.standard_normal(H) * 0.3),
        "W_aggr_f": bf(np.random.standard_normal((K, K)) / np.sqrt(K) / t[:, None]),
        "b_aggr_f": bf(np.random.standard_normal(K) * 0.3),
    }


def reference(x, x_mask, neighbour_h, neighbour_c, W_f_in, b_f_in, W_aggr_f, b_aggr_f):
    h_flat = f64(neighbour_h).reshape(N, K)
    f_input = ((mxq(f64(x), 1, "e4m3") @ mxq(f64(W_f_in), 0, "e4m3")) + f64(b_f_in)) * f64(x_mask)[:, None]
    f_input = np.tile(f_input, (1, N_CH))
    f_gate = (mxq(h_flat, 1, "e4m3") @ mxq(f64(W_aggr_f), 0, "e4m3")) + f64(b_aggr_f) + f_input
    f_aggr = f_gate + f_input
    f = sigmoid(f_aggr).reshape(N, N_CH, H)
    return np.sum(f * f64(neighbour_c), axis=1)

@@ -1,0 +1,403 @@
+from contextlib import ExitStack
+
+import concourse.mybir as mybir
+from concourse.masks import make_identity
+
+F32 = mybir.dt.float32
+BF16 = mybir.dt.bfloat16
+U32 = mybir.dt.uint32
+U8 = mybir.dt.uint8
+FP8X4 = mybir.dt.float8_e4m3fn_x4
+AF = mybir.ActivationFunctionType
+ALU = mybir.AluOpType
+
+P = 128
+NODES = 4096
+XDIM = 512
+HDIM = 256
+KIDS = 4
+KDIM = KIDS * HDIM
+CHUNK = 512
+TILES = CHUNK // P
+NCHUNK = NODES // CHUNK
+LAG = 2
+FLOPS = 2 * NODES * KDIM * KDIM + 2 * NODES * XDIM * HDIM
+
+
+def tile_treelstmcell_pa_t_kernel(
+    tc, x, x_mask, neighbour_h, neighbour_c, W_f_in, b_f_in, W_aggr_f, b_aggr_f, out
+):
+    nc = tc.nc
+    x_v = x.rearrange("(c p t) k -> c p (t k)", p=P, t=TILES)
+    h_v = neighbour_h.rearrange("(c p t) k j -> c p (t k j)", p=P, t=TILES)
+    c_v = neighbour_c.rearrange("(c p t) k j -> c p (t k j)", p=P, t=TILES)
+    o_v = out.rearrange("(c p t) j -> c p (t j)", p=P, t=TILES)
+    w_v = W_aggr_f.rearrange("(g q t) c -> g q t c", g=2, q=P, t=4)
+    wf_v = W_f_in.rearrange("(q t) c -> q (t c)", q=P, t=4)
+
+    with ExitStack() as ctx:
+        const = ctx.enter_context(tc.tile_pool(name="const", bufs=1))
+        loads = ctx.enter_context(tc.tile_pool(name="loads", bufs=3))
+        quant = ctx.enter_context(tc.tile_pool(name="quant", bufs=2))
+        work = ctx.enter_context(tc.tile_pool(name="work", bufs=2))
+        zps = ctx.enter_context(tc.psum_pool(name="zps", bufs=4))
+        fps = ctx.enter_context(tc.psum_pool(name="fps", bufs=2))
+        tps = ctx.enter_context(tc.psum_pool(name="tps", bufs=2))
+        ctx.enter_context(tc.manual_schedule())
+        banks = {"z": zps, "fb": fps, "tp": tps}
+
+        xs = {}
+        hs = {}
+        cs = {}
+        ms = {}
+
+        def load_x(c):
+            x_sb = loads.tile([P, TILES * XDIM], BF16, tag="x")
+            nc.sync.dma_start(out=x_sb[:], in_=x_v[c])
+            xs[c] = x_sb
+            m_sb = loads.tile([P, CHUNK], BF16, tag="m")
+            nc.sync.dma_start(
+                out=m_sb[:], in_=x_mask[c * CHUNK : (c + 1) * CHUNK].partition_broadcast(P)
+            )
+            ms[c] = m_sb
+
+        def load_h(c):
+            h_sb = loads.tile([P, TILES * KDIM], BF16, tag="h", bufs=2)
+            nc.sync.dma_start(out=h_sb[:], in_=h_v[c])
+            hs[c] = h_sb
+
+        def load_c(c):
+            c_sb = loads.tile([P, TILES * KDIM], BF16, tag="c")
+            nc.sync.dma_start(out=c_sb[:], in_=c_v[c])
+            cs[c] = c_sb
+
+        bias_rows = const.tile([P, P], BF16)
+        nc.vector.memset(bias_rows[:], 0.0)
+        nc.scalar.dma_start(out=bias_rows[0:8, :], in_=b_aggr_f.rearrange("(r q) -> r q", q=P))
+        nc.scalar.dma_start(out=bias_rows[8:10, :], in_=b_f_in.rearrange("(r q) -> r q", q=P))
+
+        load_x(0)
+        wf_raw = const.tile([P, 4, HDIM], BF16)
+        nc.sync.dma_start(out=wf_raw[:].rearrange("q t c -> q (t c)"), in_=wf_v)
+        load_h(0)
+        w_raw = const.tile([P, 8, KDIM], BF16)
+        for g in range(2):
+            for e in range(2):
+                rows = slice(2 * e, 2 * e + 2)
+                nc.sync.dma_start(
+                    out=w_raw[:, 4 * g + 2 * e : 4 * g + 2 * e + 2, 0:HDIM],
+                    in_=w_v[g][:, rows, 0:HDIM],
+                )
+        for g in range(2):
+            for e in range(2):
+                rows = slice(2 * e, 2 * e + 2)
+                nc.sync.dma_start(
+                    out=w_raw[:, 4 * g + 2 * e : 4 * g + 2 * e + 2, HDIM:KDIM],
+                    in_=w_v[g][:, rows, HDIM:KDIM],
+                )
+        load_x(1)
+        load_h(1)
+        load_c(0)
+        load_x(2)
+        load_c(1)
+
+        ident = const.tile([P, P], F32)
+        make_identity(nc, ident[:])
+        ident_bf = const.tile([P, P], BF16)
+        make_identity(nc, ident_bf[:])
+        bias = const.tile([P, 16], F32)
+        bf2 = const.tile([P, 2], F32)
+
+        wf_grp = const.tile([P, HDIM, 4], BF16, align_bytes=64)
+        wf_codes = const.tile([P, HDIM], U32, align_bytes=64)
+        wf_scl = const.tile([P, HDIM], U8, align_bytes=64)
+        w_grp = const.tile([P, 2, KDIM, 4], BF16, align_bytes=64)
+        w_codes = const.tile([P, 2, KDIM], U32, align_bytes=64)
+        w_scl = const.tile([P, 2, KDIM], U8, align_bytes=64)
+
+        def w_regroup(g, cb, on_vector):
+            cols = slice(cb * HDIM, (cb + 1) * HDIM)
+            src = w_raw[:, 4 * g : 4 * g + 4, cols].rearrange("q t c -> q c t")
+            if on_vector:
+                nc.vector.tensor_copy(out=w_grp[:, g, cols, :], in_=src)
+            else:
+                nc.scalar.copy(out=w_grp[:, g, cols, :], in_=src)
+
+        def w_quant(g, cb):
+            cols = slice(cb * HDIM, (cb + 1) * HDIM)
+            nc.vector.quantize_mx(
+                out=w_codes[:, g, cols].bitcast(FP8X4),
+                scales=w_scl[:, g, cols],
+                in_=w_grp[:, g, cols, :].rearrange("q c t -> q (c t)"),
+            )
+
+        grps = {}
+        codes = {}
+        tpt = {}
+
+        def tr_pe(c, op, hh, bank):
+            if op == 0:
+                words = xs[c][:].bitcast(F32)
+                wpt = XDIM // 2
+                g = 0
+            else:
+                words = hs[c][:].bitcast(F32)
+                wpt = KDIM // 2
+                g = op - 1
+            tp = banks[bank].tile([P, 2, 2 * P], F32, tag=bank)
+            for u in range(2):
+                for tt in range(2):
+                    col = (2 * hh + tt) * wpt + 2 * g * P
+                    nc.tensor.transpose(
+                        tp[:, u, tt * P : (tt + 1) * P],
+                        words[:, col + u : col + 2 * P : 2],
+                        ident[:],
+                    )
+            tpt[(c, op, hh)] = tp
+
+        def tr_cp(c, op, hh, on_vector):
+            if hh == 0:
+                grp = quant.tile([P, CHUNK * 4], BF16, tag="grp%d" % op, align_bytes=64)
+                grps[(c, op)] = grp
+            dst = grps[(c, op)][:].bitcast(F32).rearrange("p (n u) -> p n u", u=2)
+            dst = dst[:, hh * 2 * P : (hh + 1) * 2 * P, :]
+            src = tpt[(c, op, hh)][:].rearrange("p u n -> p n u")
+            if on_vector:
+                nc.vector.tensor_copy(out=dst, in_=src)
+            else:
+                nc.scalar.copy(out=dst, in_=src)
+
+        def tr_quant(c, op):
+            cd = quant.tile([P, CHUNK], U32, tag="cd%d" % op, align_bytes=64)
+            sc = quant.tile([P, CHUNK], U8, tag="sc%d" % op, align_bytes=64)
+            nc.vector.quantize_mx(out=cd[:].bitcast(FP8X4), scales=sc[:], in_=grps[(c, op)][:])
+            codes[(c, op)] = (cd, sc)
+
+        fzs = {}
+        ys = {}
+        gts = {}
+
+        def fi_pe(c, jt, bank):
+            cd, sc = codes[(c, 0)]
+            cols = slice(jt * P, (jt + 1) * P)
+            fz = banks[bank].tile([P, CHUNK], F32, tag=bank)
+            nc.tensor.matmul_mx(
+                out=fz[:],
+                lhsT=wf_codes[:, cols].bitcast(FP8X4),
+                lhsT_scale=wf_scl[:, cols],
+                rhs=cd[:].bitcast(FP8X4),
+                rhs_scale=sc[:],
+                start=True,
+                stop=True,
+            )
+            fzs[(c, jt)] = fz
+
+        def fi_y(c, jt):
+            y2 = work.tile([P, CHUNK], F32, tag="y%d" % jt)
+            nc.scalar.activation(
+                out=y2[:], in_=fzs[(c, jt)][:], func=AF.Identity, bias=bf2[:, jt : jt + 1], scale=2.0
+            )
+            ys[(c, jt)] = y2
+
+        def fi_g(c, jt, eng):
+            gt = work.tile([P, CHUNK], F32, tag="g%d" % jt)
+            eng.tensor_tensor(
+                out=gt[:].rearrange("q (t p) -> q t p", t=TILES),
+                in0=ys[(c, jt)][:].rearrange("q (t p) -> q t p", t=TILES),
+                in1=ms[c][:].rearrange("q (p t) -> q t p", t=TILES),
+                op=ALU.mult,
+            )
+            gts[(c, jt)] = gt
+
+        zts = {}
+        fts = {}
+
+        def z_pe(c, k, jt):
+            ct = 2 * k + jt
+            cols = slice(ct * P, (ct + 1) * P)
+            zp = zps.tile([P, CHUNK], F32, tag="z")
+            for g in range(2):
+                cd, sc = codes[(c, 1 + g)]
+                nc.tensor.matmul_mx(
+                    out=zp[:],
+                    lhsT=w_codes[:, g, cols].bitcast(FP8X4),
+                    lhsT_scale=w_scl[:, g, cols],
+                    rhs=cd[:].bitcast(FP8X4),
+                    rhs_scale=sc[:],
+                    start=(g == 0),
+                    stop=(g == 1),
+                )
+            zts[(c, ct)] = zp
+
+        def gate(c, k, jt):
+            ct = 2 * k + jt
+            u_sb = work.tile([P, CHUNK], F32, tag="u", bufs=4)
+            nc.vector.tensor_tensor(out=u_sb[:], in0=zts[(c, ct)][:], in1=gts[(c, jt)][:], op=ALU.add)
+            f_sb = work.tile([P, CHUNK], F32, tag="f", bufs=10)
+            nc.scalar.activation(
+                out=f_sb[:], in_=u_sb[:], func=AF.Sigmoid, bias=bias[:, ct : ct + 1], scale=1.0
+            )
+            fts[(c, ct)] = f_sb
+
+        fbs = {}
+        prods = {}
+        accs = {}
+
+        def fb_pe(c, k, hh):
+            fb = fps.tile([P, 2, HDIM], F32, tag="fb")
+            for tt in range(2):
+                t = 2 * hh + tt
+                for jt in range(2):
+                    nc.tensor.transpose(
+                        fb[:, tt, jt * P : (jt + 1) * P],
+                        fts[(c, 2 * k + jt)][:, t * P : (t + 1) * P],
+                        ident[:],
+                    )
+            fbs[(c, k, hh)] = fb
+
+        def times_c(c, k, hh):
+            if hh == 0:
+                prod = work.tile([P, TILES, HDIM], F32, tag="prod", bufs=4)
+                prods[(c, k)] = prod
+            half = slice(2 * hh, 2 * hh + 2)
+            c4 = cs[c][:].rearrange("p (t k j) -> p t k j", t=TILES, k=KIDS)
+            nc.vector.tensor_tensor(
+                out=prods[(c, k)][:, half, :], in0=fbs[(c, k, hh)][:], in1=c4[:, half, k, :], op=ALU.mult
+            )
+
+        def finish(c, k):
+            last = c == NCHUNK - 1
+            for hh in range(2):
+                times_c(c, k, hh)
+                if last and k == 3:
+                    half = slice(2 * hh, 2 * hh + 2)
+                    nc.vector.tensor_tensor(
+                        out=prods[(c, 3)][:, half, :],
+                        in0=prods[(c, 3)][:, half, :],
+                        in1=prods[(c, 2)][:, half, :],
+                        op=ALU.add,
+                    )
+                    nc.vector.tensor_tensor(
+                        out=accs[c][:, half, :],
+                        in0=accs[c][:, half, :],
+                        in1=prods[(c, 3)][:, half, :],
+                        op=ALU.add,
+                    )
+                    nc.sync.dma_start(
+                        out=o_v[c][:, hh * 2 * HDIM : (hh + 1) * 2 * HDIM],
+                        in_=accs[c][:, half, :].rearrange("p t j -> p (t j)"),
+                    )
+            if k == 1:
+                acc = work.tile([P, TILES, HDIM], F32, tag="acc")
+                nc.gpsimd.tensor_tensor(
+                    out=acc[:], in0=prods[(c, 0)][:], in1=prods[(c, 1)][:], op=ALU.add
+                )
+                accs[c] = acc
+            elif k >= 2 and not last:
+                nc.gpsimd.tensor_tensor(
+                    out=accs[c][:], in0=accs[c][:], in1=prods[(c, k)][:], op=ALU.add
+                )
+                if k == 3:
+                    nc.sync.dma_start(out=o_v[c], in_=accs[c][:].rearrange("p t j -> p (t j)"))
+
+        nc.vector.tensor_copy(out=wf_grp[:], in_=wf_raw[:].rearrange("q t c -> q c t"))
+        tr_pe(0, 0, 0, "tp")
+        tr_pe(0, 0, 1, "tp")
+        tr_cp(0, 0, 0, False)
+        tr_cp(0, 0, 1, True)
+        nc.vector.quantize_mx(
+            out=wf_codes[:].bitcast(FP8X4),
+            scales=wf_scl[:],
+            in_=wf_grp[:].rearrange("q c t -> q (c t)"),
+        )
+        tr_quant(0, 0)
+        tr_pe(0, 1, 0, "fb")
+        tr_pe(0, 1, 1, "fb")
+        tr_pe(0, 2, 0, "z")
+        tr_pe(0, 2, 1, "z")
+        bias_ps = tps.tile([P, P], BF16, tag="tp")
+        nc.tensor.transpose(bias_ps[:], bias_rows[:], ident_bf[:])
+        nc.vector.tensor_copy(out=bias[:, 0:10], in_=bias_ps[:, 0:10])
+        nc.vector.tensor_scalar_mul(out=bf2[:], in0=bias[:, 8:10], scalar1=2.0)
+        tr_cp(0, 1, 0, False)
+        tr_cp(0, 1, 1, True)
+        tr_cp(0, 2, 0, False)
+        tr_cp(0, 2, 1, True)
+        fi_pe(0, 0, "z")
+        fi_pe(0, 1, "z")
+        fi_y(0, 0)
+        fi_y(0, 1)
+        w_regroup(0, 0, True)
+        w_regroup(1, 0, True)
+        tr_quant(0, 1)
+        w_quant(0, 0)
+        w_quant(1, 0)
+        tr_quant(0, 2)
+        w_regroup(0, 1, True)
+        w_regroup(1, 1, True)
+        for cb in range(2, 4):
+            w_regroup(0, cb, False)
+            w_regroup(1, cb, False)
+        w_quant(0, 1)
+        w_quant(1, 1)
+        fi_g(0, 0, nc.vector)
+        fi_g(0, 1, nc.vector)
+
+        total = NCHUNK * KIDS
+        for i in range(total + LAG):
+            c, j = divmod(i, KIDS)
+            live = i < total
+            units = []
+            if live:
+                if i == 0:
+                    units.append((1, 0))
+                if j == 0 and c + 1 < NCHUNK:
+                    units.append((c + 1, 1))
+                if j == 1 and c + 1 < NCHUNK:
+                    units.append((c + 1, 2))
+                if j == 3 and c + 2 < NCHUNK:
+                    units.append((c + 2, 0))
+            fi_now = live and j == 2 and c + 1 < NCHUNK
+            if live:
+                z_pe(c, j, 0)
+                z_pe(c, j, 1)
+            if fi_now:
+                fi_pe(c + 1, 0, "tp")
+                fi_pe(c + 1, 1, "tp")
+            for cc, op in units:
+                tr_pe(cc, op, 0, "tp")
+                tr_pe(cc, op, 1, "tp")
+            if i >= LAG:
+                c2, k2 = divmod(i - LAG, KIDS)
+                fb_pe(c2, k2, 0)
+                fb_pe(c2, k2, 1)
+            if live and j == 0:
+                if c + 2 < NCHUNK:
+                    load_h(c + 2)
+                if c + 3 < NCHUNK:
+                    load_x(c + 3)
+                if i == 0:
+                    load_c(2)
+            if fi_now:
+                for jt in range(2):
+                    fi_y(c + 1, jt)
+                    fi_g(c + 1, jt, nc.gpsimd)
+            for cc, op in units:
+                tr_cp(cc, op, 0, False)
+                tr_cp(cc, op, 1, False)
+            if live:
+                gate(c, j, 0)
+                gate(c, j, 1)
+            if i >= LAG:
+                c2, k2 = divmod(i - LAG, KIDS)
+                finish(c2, k2)
+                if k2 == 3 and c2 + 3 < NCHUNK:
+                    load_c(c2 + 3)
+            if live:
+                if c == 0 and j < 2:
+                    w_quant(0, j + 2)
+                    w_quant(1, j + 2)
+                if i == 1:
+                    tr_quant(1, 0)
+                if c + 1 < NCHUNK and j < 3 and i > 0:
+                    tr_quant(c + 1, j)

@@ -55,20 +55,17 @@ def tile_treelstmcell_pa_t_kernel(
             x_sb = loads.tile([P, TILES * XDIM], BF16, tag="x")
             nc.sync.dma_start(out=x_sb[:], in_=x_v[c])
             xs[c] = x_sb
-            m_sb = loads.tile([P, CHUNK], BF16, tag="m")
-            nc.sync.dma_start(
-                out=m_sb[:], in_=x_mask[c * CHUNK : (c + 1) * CHUNK].partition_broadcast(P)
-            )
-            ms[c] = m_sb
 
         def load_h(c):
             h_sb = loads.tile([P, TILES * KDIM], BF16, tag="h", bufs=2)
-            nc.sync.dma_start(out=h_sb[:], in_=h_v[c])
+            for a in range(0, TILES * KDIM, 2 * KDIM):
+                nc.sync.dma_start(out=h_sb[:, a : a + 2 * KDIM], in_=h_v[c][:, a : a + 2 * KDIM])
             hs[c] = h_sb
 
         def load_c(c):
             c_sb = loads.tile([P, TILES * KDIM], BF16, tag="c")
-            nc.sync.dma_start(out=c_sb[:], in_=c_v[c])
+            for a in range(0, TILES * KDIM, 2 * KDIM):
+                nc.sync.dma_start(out=c_sb[:, a : a + 2 * KDIM], in_=c_v[c][:, a : a + 2 * KDIM])
             cs[c] = c_sb
 
         bias_rows = const.tile([P, P], BF16)
@@ -76,30 +73,38 @@ def tile_treelstmcell_pa_t_kernel(
         nc.scalar.dma_start(out=bias_rows[0:8, :], in_=b_aggr_f.rearrange("(r q) -> r q", q=P))
         nc.scalar.dma_start(out=bias_rows[8:10, :], in_=b_f_in.rearrange("(r q) -> r q", q=P))
 
+        m_row = const.tile([P, CHUNK], BF16)
+        nc.gpsimd.memset(m_row[:].bitcast(U32), 0)
+        nc.scalar.dma_start(out=m_row[0:1, :], in_=x_mask[0:CHUNK].rearrange("(o n) -> o n", o=1))
+        ones = const.tile([P, P], BF16)
+        nc.gpsimd.memset(ones[:], 1.0)
+        m_all = const.tile([P, NODES], BF16)
+        m_first = const.tile([P, CHUNK], BF16)
+        ms[0] = m_first[:]
+        for c in range(1, NCHUNK):
+            ms[c] = m_all[:, c * CHUNK : (c + 1) * CHUNK]
+
         load_x(0)
         wf_raw = const.tile([P, 4, HDIM], BF16)
         nc.sync.dma_start(out=wf_raw[:].rearrange("q t c -> q (t c)"), in_=wf_v)
-        load_h(0)
         w_raw = const.tile([P, 8, KDIM], BF16)
-        for g in range(2):
-            for e in range(2):
-                rows = slice(2 * e, 2 * e + 2)
-                nc.sync.dma_start(
-                    out=w_raw[:, 4 * g + 2 * e : 4 * g + 2 * e + 2, 0:HDIM],
-                    in_=w_v[g][:, rows, 0:HDIM],
-                )
-        for g in range(2):
-            for e in range(2):
-                rows = slice(2 * e, 2 * e + 2)
-                nc.sync.dma_start(
-                    out=w_raw[:, 4 * g + 2 * e : 4 * g + 2 * e + 2, HDIM:KDIM],
-                    in_=w_v[g][:, rows, HDIM:KDIM],
-                )
+
+        def load_w(c0, c1):
+            for g in range(2):
+                nc.sync.dma_start(out=w_raw[:, 4 * g : 4 * g + 4, c0:c1], in_=w_v[g][:, :, c0:c1])
+
+        load_w(0, HDIM)
+        load_h(0)
+        load_w(HDIM, 2 * HDIM)
+        load_w(2 * HDIM, KDIM)
         load_x(1)
         load_h(1)
         load_c(0)
-        load_x(2)
+        nc.sync.dma_start(
+            out=m_all[:, CHUNK:NODES], in_=x_mask[CHUNK:NODES].partition_broadcast(P)
+        )
         load_c(1)
+        load_x(2)
 
         ident = const.tile([P, P], F32)
         make_identity(nc, ident[:])
@@ -115,13 +120,20 @@ def tile_treelstmcell_pa_t_kernel(
         w_codes = const.tile([P, 2, KDIM], U32, align_bytes=64)
         w_scl = const.tile([P, 2, KDIM], U8, align_bytes=64)
 
-        def w_regroup(g, cb, on_vector):
+        def regroup(eng, dst, src, factor):
+            if eng == "v":
+                nc.vector.tensor_copy(out=dst, in_=src)
+            elif eng == "s":
+                nc.scalar.copy(out=dst, in_=src)
+            else:
+                nc.gpsimd.tensor_scalar(
+                    out=dst, in0=src, scalar1=factor, scalar2=0.0, op0=ALU.mult, op1=ALU.add
+                )
+
+        def w_regroup(g, cb, eng):
             cols = slice(cb * HDIM, (cb + 1) * HDIM)
             src = w_raw[:, 4 * g : 4 * g + 4, cols].rearrange("q t c -> q c t")
-            if on_vector:
-                nc.vector.tensor_copy(out=w_grp[:, g, cols, :], in_=src)
-            else:
-                nc.scalar.copy(out=w_grp[:, g, cols, :], in_=src)
+            regroup(eng, w_grp[:, g, cols, :], src, 1.0)
 
         def w_quant(g, cb):
             cols = slice(cb * HDIM, (cb + 1) * HDIM)
@@ -148,11 +160,8 @@ def tile_treelstmcell_pa_t_kernel(
             for u in range(2):
                 for tt in range(2):
                     col = (2 * hh + tt) * wpt + 2 * g * P
-                    nc.tensor.transpose(
-                        tp[:, u, tt * P : (tt + 1) * P],
-                        words[:, col + u : col + 2 * P : 2],
-                        ident[:],
-                    )
+                    src = words[:, col + u : col + 2 * P : 2]
+                    nc.tensor.transpose(tp[:, u, tt * P : (tt + 1) * P], src, ident[:])
             tpt[(c, op, hh)] = tp
 
         def tr_cp(c, op, hh, on_vector):
@@ -195,19 +204,31 @@ def tile_treelstmcell_pa_t_kernel(
         def fi_y(c, jt):
             y2 = work.tile([P, CHUNK], F32, tag="y%d" % jt)
             nc.scalar.activation(
-                out=y2[:], in_=fzs[(c, jt)][:], func=AF.Identity, bias=bf2[:, jt : jt + 1], scale=2.0
+                out=y2[:], in_=fzs[(c, jt)][:], func=AF.Identity, bias=bf2[:, jt : jt + 1], scale=1.0
             )
             ys[(c, jt)] = y2
 
-        def fi_g(c, jt, eng):
+        def fi_g(c, jt):
             gt = work.tile([P, CHUNK], F32, tag="g%d" % jt)
-            eng.tensor_tensor(
+            nc.gpsimd.tensor_tensor(
                 out=gt[:].rearrange("q (t p) -> q t p", t=TILES),
                 in0=ys[(c, jt)][:].rearrange("q (t p) -> q t p", t=TILES),
-                in1=ms[c][:].rearrange("q (p t) -> q t p", t=TILES),
+                in1=ms[c].rearrange("q (p t) -> q t p", t=TILES),
                 op=ALU.mult,
             )
             gts[(c, jt)] = gt
+
+        def fi_first(jt):
+            gt = work.tile([P, CHUNK], F32, tag="g%d" % jt)
+            nc.vector.scalar_tensor_tensor(
+                out=gt[:].rearrange("q (t p) -> q t p", t=TILES),
+                in0=fzs[(0, jt)][:].rearrange("q (t p) -> q t p", t=TILES),
+                scalar=bf2[:, jt : jt + 1],
+                in1=ms[0].rearrange("q (p t) -> q t p", t=TILES),
+                op0=ALU.add,
+                op1=ALU.mult,
+            )
+            gts[(0, jt)] = gt
 
         zts = {}
         fts = {}
@@ -265,99 +286,106 @@ def tile_treelstmcell_pa_t_kernel(
                 out=prods[(c, k)][:, half, :], in0=fbs[(c, k, hh)][:], in1=c4[:, half, k, :], op=ALU.mult
             )
 
-        def finish(c, k):
-            last = c == NCHUNK - 1
-            for hh in range(2):
-                times_c(c, k, hh)
-                if last and k == 3:
-                    half = slice(2 * hh, 2 * hh + 2)
-                    nc.vector.tensor_tensor(
-                        out=prods[(c, 3)][:, half, :],
-                        in0=prods[(c, 3)][:, half, :],
-                        in1=prods[(c, 2)][:, half, :],
-                        op=ALU.add,
-                    )
-                    nc.vector.tensor_tensor(
-                        out=accs[c][:, half, :],
-                        in0=accs[c][:, half, :],
-                        in1=prods[(c, 3)][:, half, :],
-                        op=ALU.add,
-                    )
+        def add(eng, c, k, half):
+            acc = accs[c][:, half, :]
+            first = prods[(c, 0)][:, half, :] if k == 1 else acc
+            eng.tensor_tensor(out=acc, in0=first, in1=prods[(c, k)][:, half, :], op=ALU.add)
+
+        def finish_last(k):
+            c = NCHUNK - 1
+            halves = (slice(0, 2), slice(2, 4))
+            if k == 1:
+                add(nc.gpsimd, c, 1, halves[0])
+                add(nc.gpsimd, c, 1, halves[1])
+            if k == 2:
+                add(nc.gpsimd, c, 2, halves[1])
+            if k == 3:
+                p3 = prods[(c, 3)][:, halves[0], :]
+                nc.vector.tensor_tensor(out=p3, in0=p3, in1=prods[(c, 2)][:, halves[0], :], op=ALU.add)
+                for hh in range(2):
+                    add(nc.vector, c, 3, halves[hh])
                     nc.sync.dma_start(
                         out=o_v[c][:, hh * 2 * HDIM : (hh + 1) * 2 * HDIM],
-                        in_=accs[c][:, half, :].rearrange("p t j -> p (t j)"),
+                        in_=accs[c][:, halves[hh], :].rearrange("p t j -> p (t j)"),
                     )
+
+        def finish(c, k):
+            last = c == NCHUNK - 1
             if k == 1:
                 acc = work.tile([P, TILES, HDIM], F32, tag="acc")
-                nc.gpsimd.tensor_tensor(
-                    out=acc[:], in0=prods[(c, 0)][:], in1=prods[(c, 1)][:], op=ALU.add
-                )
                 accs[c] = acc
-            elif k >= 2 and not last:
-                nc.gpsimd.tensor_tensor(
-                    out=accs[c][:], in0=accs[c][:], in1=prods[(c, k)][:], op=ALU.add
-                )
-                if k == 3:
-                    nc.sync.dma_start(out=o_v[c], in_=accs[c][:].rearrange("p t j -> p (t j)"))
+            for hh in range(2):
+                times_c(c, k, hh)
+            if last:
+                finish_last(k)
+                return
+            if k >= 1:
+                add(nc.gpsimd, c, k, slice(0, TILES))
+            if k == 3:
+                nc.sync.dma_start(out=o_v[c], in_=accs[c][:].rearrange("p t j -> p (t j)"))
 
-        nc.vector.tensor_copy(out=wf_grp[:], in_=wf_raw[:].rearrange("q t c -> q c t"))
+        warm = const.tile([P, 1], F32)
+        nc.vector.memset(warm[:], 0.0)
+        nc.scalar.activation(out=warm[:], in_=warm[:], func=AF.Sigmoid)
+        regroup("g", wf_grp[:], wf_raw[:].rearrange("q t c -> q c t"), 2.0)
         tr_pe(0, 0, 0, "tp")
         tr_pe(0, 0, 1, "tp")
         tr_cp(0, 0, 0, False)
         tr_cp(0, 0, 1, True)
+        tr_quant(0, 0)
         nc.vector.quantize_mx(
             out=wf_codes[:].bitcast(FP8X4),
             scales=wf_scl[:],
             in_=wf_grp[:].rearrange("q c t -> q (c t)"),
         )
-        tr_quant(0, 0)
         tr_pe(0, 1, 0, "fb")
-        tr_pe(0, 1, 1, "fb")
-        tr_pe(0, 2, 0, "z")
-        tr_pe(0, 2, 1, "z")
-        bias_ps = tps.tile([P, P], BF16, tag="tp")
+        tr_pe(0, 2, 0, "fb")
+        bias_ps = zps.tile([P, P], BF16, tag="z")
         nc.tensor.transpose(bias_ps[:], bias_rows[:], ident_bf[:])
-        nc.vector.tensor_copy(out=bias[:, 0:10], in_=bias_ps[:, 0:10])
-        nc.vector.tensor_scalar_mul(out=bf2[:], in0=bias[:, 8:10], scalar1=2.0)
-        tr_cp(0, 1, 0, False)
-        tr_cp(0, 1, 1, True)
-        tr_cp(0, 2, 0, False)
-        tr_cp(0, 2, 1, True)
-        fi_pe(0, 0, "z")
-        fi_pe(0, 1, "z")
-        fi_y(0, 0)
-        fi_y(0, 1)
-        w_regroup(0, 0, True)
-        w_regroup(1, 0, True)
-        tr_quant(0, 1)
+        m_ps = zps.tile([P, CHUNK], F32, tag="z")
+        nc.tensor.matmul(m_ps[:], lhsT=ones[:], rhs=m_row[:], start=True, stop=True)
+        tr_pe(0, 1, 1, "z")
+        tr_pe(0, 2, 1, "z")
+        fi_pe(0, 0, "tp")
+        fi_pe(0, 1, "tp")
+        w_regroup(0, 0, "g")
+        w_regroup(1, 0, "s")
         w_quant(0, 0)
         w_quant(1, 0)
+        tr_cp(0, 1, 0, False)
+        tr_cp(0, 2, 0, True)
+        nc.scalar.copy(out=m_first[:], in_=m_ps[:])
+        nc.vector.tensor_copy(out=bias[:, 0:10], in_=bias_ps[:, 0:10])
+        nc.vector.tensor_scalar_mul(out=bf2[:], in0=bias[:, 8:10], scalar1=2.0)
+        tr_cp(0, 1, 1, False)
+        tr_cp(0, 2, 1, True)
+        tr_quant(0, 1)
         tr_quant(0, 2)
-        w_regroup(0, 1, True)
-        w_regroup(1, 1, True)
-        for cb in range(2, 4):
-            w_regroup(0, cb, False)
-            w_regroup(1, cb, False)
-        w_quant(0, 1)
-        w_quant(1, 1)
-        fi_g(0, 0, nc.vector)
-        fi_g(0, 1, nc.vector)
+        fi_first(0)
+        fi_first(1)
+        for cb in range(1, 4):
+            w_regroup(0, cb, "g")
+            w_regroup(1, cb, "s")
 
         total = NCHUNK * KIDS
         for i in range(total + LAG):
             c, j = divmod(i, KIDS)
             live = i < total
             units = []
-            if live:
-                if i == 0:
-                    units.append((1, 0))
-                if j == 0 and c + 1 < NCHUNK:
-                    units.append((c + 1, 1))
-                if j == 1 and c + 1 < NCHUNK:
-                    units.append((c + 1, 2))
+            early = []
+            quants = []
+            if i < KIDS:
+                units = [[(1, 0)], [(1, 1)], [(1, 2)], [(2, 0)]][i]
+                early = [[], [], [], [(1, 2)]][i]
+                quants = [[], [(1, 0)], [(1, 1)], []][i]
+            elif live:
+                if j < 2 and c + 1 < NCHUNK:
+                    units.append((c + 1, j + 1))
                 if j == 3 and c + 2 < NCHUNK:
                     units.append((c + 2, 0))
-            fi_now = live and j == 2 and c + 1 < NCHUNK
+                if j < 3 and c + 1 < NCHUNK:
+                    quants.append((c + 1, j))
+            fi_now = live and c + 1 < NCHUNK and j == 2
             if live:
                 z_pe(c, j, 0)
                 z_pe(c, j, 1)
@@ -381,23 +409,22 @@ def tile_treelstmcell_pa_t_kernel(
             if fi_now:
                 for jt in range(2):
                     fi_y(c + 1, jt)
-                    fi_g(c + 1, jt, nc.gpsimd)
+                    fi_g(c + 1, jt)
             for cc, op in units:
                 tr_cp(cc, op, 0, False)
                 tr_cp(cc, op, 1, False)
             if live:
                 gate(c, j, 0)
+                if i < 3:
+                    w_quant(0, i + 1)
+                    w_quant(1, i + 1)
                 gate(c, j, 1)
+            for cc, op in early:
+                tr_quant(cc, op)
             if i >= LAG:
                 c2, k2 = divmod(i - LAG, KIDS)
                 finish(c2, k2)
                 if k2 == 3 and c2 + 3 < NCHUNK:
                     load_c(c2 + 3)
-            if live:
-                if c == 0 and j < 2:
-                    w_quant(0, j + 2)
-                    w_quant(1, j + 2)
-                if i == 1:
-                    tr_quant(1, 0)
-                if c + 1 < NCHUNK and j < 3 and i > 0:
-                    tr_quant(c + 1, j)
+            for cc, op in quants:
+                tr_quant(cc, op)

@@ -252,11 +252,10 @@ def tile_treelstmcell_pa_t_kernel(
 
         def gate(c, k, jt):
             ct = 2 * k + jt
-            u_sb = work.tile([P, CHUNK], F32, tag="u", bufs=4)
-            nc.vector.tensor_tensor(out=u_sb[:], in0=zts[(c, ct)][:], in1=gts[(c, jt)][:], op=ALU.add)
-            f_sb = work.tile([P, CHUNK], F32, tag="f", bufs=10)
+            f_sb = work.tile([P, CHUNK], F32, tag="f", bufs=12)
+            nc.vector.tensor_tensor(out=f_sb[:], in0=zts[(c, ct)][:], in1=gts[(c, jt)][:], op=ALU.add)
             nc.scalar.activation(
-                out=f_sb[:], in_=u_sb[:], func=AF.Sigmoid, bias=bias[:, ct : ct + 1], scale=1.0
+                out=f_sb[:], in_=f_sb[:], func=AF.Sigmoid, bias=bias[:, ct : ct + 1], scale=1.0
             )
             fts[(c, ct)] = f_sb
 
@@ -277,8 +276,8 @@ def tile_treelstmcell_pa_t_kernel(
             fbs[(c, k, hh)] = fb
 
         def times_c(c, k, hh):
-            if hh == 0:
-                prod = work.tile([P, TILES, HDIM], F32, tag="prod", bufs=4)
+            if (c, k) not in prods:
+                prod = work.tile([P, TILES, HDIM], F32, tag="prod", bufs=8)
                 prods[(c, k)] = prod
             half = slice(2 * hh, 2 * hh + 2)
             c4 = cs[c][:].rearrange("p (t k j) -> p t k j", t=TILES, k=KIDS)

@@ -323,12 +323,22 @@ def tile_treelstmcell_pa_t_kernel(
             if k == 3:
                 nc.sync.dma_start(out=o_v[c], in_=accs[c][:].rearrange("p t j -> p (t j)"))
 
+        idle_in = const.tile([P, CHUNK], BF16)
+        nc.vector.memset(idle_in[:].bitcast(U32), 0)
+
+        def spin(n):
+            idle_out = fps.tile([P, CHUNK], F32, tag="fb")
+            for i in range(n):
+                nc.tensor.matmul(idle_out[:], lhsT=idle_in[:, 0:P], rhs=idle_in[:], start=True, stop=True)
+
+        spin(5)
         warm = const.tile([P, 1], F32)
         nc.vector.memset(warm[:], 0.0)
         nc.scalar.activation(out=warm[:], in_=warm[:], func=AF.Sigmoid)
         regroup("g", wf_grp[:], wf_raw[:].rearrange("q t c -> q c t"), 2.0)
         tr_pe(0, 0, 0, "tp")
         tr_pe(0, 0, 1, "tp")
+        spin(2)
         tr_cp(0, 0, 0, False)
         tr_cp(0, 0, 1, True)
         tr_quant(0, 0)
@@ -347,6 +357,7 @@ def tile_treelstmcell_pa_t_kernel(
         tr_pe(0, 2, 1, "z")
         fi_pe(0, 0, "tp")
         fi_pe(0, 1, "tp")
+        spin(2)
         w_regroup(0, 0, "g")
         w_regroup(1, 0, "s")
         w_quant(0, 0)

@@ -40,8 +40,8 @@ def tile_treelstmcell_pa_t_kernel(
         loads = ctx.enter_context(tc.tile_pool(name="loads", bufs=3))
         quant = ctx.enter_context(tc.tile_pool(name="quant", bufs=2))
         work = ctx.enter_context(tc.tile_pool(name="work", bufs=2))
-        zps = ctx.enter_context(tc.psum_pool(name="zps", bufs=4))
-        fps = ctx.enter_context(tc.psum_pool(name="fps", bufs=2))
+        zps = ctx.enter_context(tc.psum_pool(name="zps", bufs=3))
+        fps = ctx.enter_context(tc.psum_pool(name="fps", bufs=3))
         tps = ctx.enter_context(tc.psum_pool(name="tps", bufs=2))
         ctx.enter_context(tc.manual_schedule())
         banks = {"z": zps, "fb": fps, "tp": tps}
@@ -103,8 +103,8 @@ def tile_treelstmcell_pa_t_kernel(
         nc.sync.dma_start(
             out=m_all[:, CHUNK:NODES], in_=x_mask[CHUNK:NODES].partition_broadcast(P)
         )
-        load_c(1)
         load_x(2)
+        load_c(1)
 
         ident = const.tile([P, P], F32)
         make_identity(nc, ident[:])

@@ -64,8 +64,9 @@ def tile_treelstmcell_pa_t_kernel(
 
         def load_c(c):
             c_sb = loads.tile([P, TILES * KDIM], BF16, tag="c")
-            for a in range(0, TILES * KDIM, 2 * KDIM):
-                nc.sync.dma_start(out=c_sb[:, a : a + 2 * KDIM], in_=c_v[c][:, a : a + 2 * KDIM])
+            step = (2 if c == 0 else TILES) * KDIM
+            for a in range(0, TILES * KDIM, step):
+                nc.sync.dma_start(out=c_sb[:, a : a + step], in_=c_v[c][:, a : a + step])
             cs[c] = c_sb
 
         bias_rows = const.tile([P, P], BF16)
@@ -147,6 +148,17 @@ def tile_treelstmcell_pa_t_kernel(
         codes = {}
         tpt = {}
 
+        pxs = {}
+
+        def perm(c, op):
+            words = (xs if op == 0 else hs)[c][:].bitcast(F32).rearrange("p (t w) -> p t w", t=TILES)
+            px = quant.tile([P, TILES, 2, P], F32, tag="px%d" % op, bufs=1)
+            first = max(op - 1, 0) * 2 * P
+            nc.scalar.copy(
+                out=px[:], in_=words[:, :, first : first + 2 * P].rearrange("p t (w u) -> p t u w", u=2)
+            )
+            pxs[(c, op)] = px
+
         def tr_pe(c, op, hh, bank):
             if op == 0:
                 words = xs[c][:].bitcast(F32)
@@ -161,6 +173,8 @@ def tile_treelstmcell_pa_t_kernel(
                 for tt in range(2):
                     col = (2 * hh + tt) * wpt + 2 * g * P
                     src = words[:, col + u : col + 2 * P : 2]
+                    if (c, op) in pxs:
+                        src = pxs[(c, op)][:, 2 * hh + tt, u, :]
                     nc.tensor.transpose(tp[:, u, tt * P : (tt + 1) * P], src, ident[:])
             tpt[(c, op, hh)] = tp
 
@@ -363,12 +377,12 @@ def tile_treelstmcell_pa_t_kernel(
         w_quant(0, 0)
         w_quant(1, 0)
         tr_cp(0, 1, 0, False)
-        tr_cp(0, 2, 0, True)
+        tr_cp(0, 2, 0, False)
         nc.scalar.copy(out=m_first[:], in_=m_ps[:])
         nc.vector.tensor_copy(out=bias[:, 0:10], in_=bias_ps[:, 0:10])
         nc.vector.tensor_scalar_mul(out=bf2[:], in0=bias[:, 8:10], scalar1=2.0)
         tr_cp(0, 1, 1, False)
-        tr_cp(0, 2, 1, True)
+        tr_cp(0, 2, 1, False)
         tr_quant(0, 1)
         tr_quant(0, 2)
         fi_first(0)
@@ -416,6 +430,8 @@ def tile_treelstmcell_pa_t_kernel(
                     load_x(c + 3)
                 if i == 0:
                     load_c(2)
+            if live and i >= 3 and j == 2 and c + 2 < NCHUNK:
+                perm(c + 2, 0)
             if fi_now:
                 for jt in range(2):
                     fi_y(c + 1, jt)

from contextlib import ExitStack

import concourse.mybir as mybir
from concourse.masks import make_identity

F32 = mybir.dt.float32
BF16 = mybir.dt.bfloat16
U32 = mybir.dt.uint32
U8 = mybir.dt.uint8
FP8X4 = mybir.dt.float8_e4m3fn_x4
AF = mybir.ActivationFunctionType
ALU = mybir.AluOpType

P = 128
NODES = 4096
XDIM = 512
HDIM = 256
KIDS = 4
KDIM = KIDS * HDIM
CHUNK = 512
TILES = CHUNK // P
NCHUNK = NODES // CHUNK
LAG = 2
FLOPS = 2 * NODES * KDIM * KDIM + 2 * NODES * XDIM * HDIM


def tile_treelstmcell_pa_t_kernel(
    tc, x, x_mask, neighbour_h, neighbour_c, W_f_in, b_f_in, W_aggr_f, b_aggr_f, out
):
    nc = tc.nc
    x_v = x.rearrange("(c p t) k -> c p (t k)", p=P, t=TILES)
    h_v = neighbour_h.rearrange("(c p t) k j -> c p (t k j)", p=P, t=TILES)
    c_v = neighbour_c.rearrange("(c p t) k j -> c p (t k j)", p=P, t=TILES)
    o_v = out.rearrange("(c p t) j -> c p (t j)", p=P, t=TILES)
    w_v = W_aggr_f.rearrange("(g q t) c -> g q t c", g=2, q=P, t=4)
    wf_v = W_f_in.rearrange("(q t) c -> q (t c)", q=P, t=4)

    with ExitStack() as ctx:
        const = ctx.enter_context(tc.tile_pool(name="const", bufs=1))
        loads = ctx.enter_context(tc.tile_pool(name="loads", bufs=3))
        quant = ctx.enter_context(tc.tile_pool(name="quant", bufs=2))
        work = ctx.enter_context(tc.tile_pool(name="work", bufs=2))
        zps = ctx.enter_context(tc.psum_pool(name="zps", bufs=3))
        fps = ctx.enter_context(tc.psum_pool(name="fps", bufs=3))
        tps = ctx.enter_context(tc.psum_pool(name="tps", bufs=2))
        ctx.enter_context(tc.manual_schedule())
        banks = {"z": zps, "fb": fps, "tp": tps}

        xs = {}
        hs = {}
        cs = {}
        ms = {}

        def load_x(c):
            x_sb = loads.tile([P, TILES * XDIM], BF16, tag="x")
            nc.sync.dma_start(out=x_sb[:], in_=x_v[c])
            xs[c] = x_sb

        def load_h(c):
            h_sb = loads.tile([P, TILES * KDIM], BF16, tag="h", bufs=2)
            for a in range(0, TILES * KDIM, 2 * KDIM):
                nc.sync.dma_start(out=h_sb[:, a : a + 2 * KDIM], in_=h_v[c][:, a : a + 2 * KDIM])
            hs[c] = h_sb

        def load_c(c):
            c_sb = loads.tile([P, TILES * KDIM], BF16, tag="c")
            step = (2 if c == 0 else TILES) * KDIM
            for a in range(0, TILES * KDIM, step):
                nc.sync.dma_start(out=c_sb[:, a : a + step], in_=c_v[c][:, a : a + step])
            cs[c] = c_sb

        bias_rows = const.tile([P, P], BF16)
        nc.vector.memset(bias_rows[:], 0.0)
        nc.scalar.dma_start(out=bias_rows[0:8, :], in_=b_aggr_f.rearrange("(r q) -> r q", q=P))
        nc.scalar.dma_start(out=bias_rows[8:10, :], in_=b_f_in.rearrange("(r q) -> r q", q=P))

        m_row = const.tile([P, CHUNK], BF16)
        nc.gpsimd.memset(m_row[:].bitcast(U32), 0)
        nc.scalar.dma_start(out=m_row[0:1, :], in_=x_mask[0:CHUNK].rearrange("(o n) -> o n", o=1))
        ones = const.tile([P, P], BF16)
        nc.gpsimd.memset(ones[:], 1.0)
        m_all = const.tile([P, NODES], BF16)
        m_first = const.tile([P, CHUNK], BF16)
        ms[0] = m_first[:]
        for c in range(1, NCHUNK):
            ms[c] = m_all[:, c * CHUNK : (c + 1) * CHUNK]

        load_x(0)
        wf_raw = const.tile([P, 4, HDIM], BF16)
        nc.sync.dma_start(out=wf_raw[:].rearrange("q t c -> q (t c)"), in_=wf_v)
        w_raw = const.tile([P, 8, KDIM], BF16)

        def load_w(c0, c1):
            for g in range(2):
                nc.sync.dma_start(out=w_raw[:, 4 * g : 4 * g + 4, c0:c1], in_=w_v[g][:, :, c0:c1])

        load_w(0, HDIM)
        load_h(0)
        load_w(HDIM, 2 * HDIM)
        load_w(2 * HDIM, KDIM)
        load_x(1)
        load_h(1)
        load_c(0)
        nc.sync.dma_start(
            out=m_all[:, CHUNK:NODES], in_=x_mask[CHUNK:NODES].partition_broadcast(P)
        )
        load_x(2)
        load_c(1)

        ident = const.tile([P, P], F32)
        make_identity(nc, ident[:])
        ident_bf = const.tile([P, P], BF16)
        make_identity(nc, ident_bf[:])
        bias = const.tile([P, 16], F32)
        bf2 = const.tile([P, 2], F32)

        wf_grp = const.tile([P, HDIM, 4], BF16, align_bytes=64)
        wf_codes = const.tile([P, HDIM], U32, align_bytes=64)
        wf_scl = const.tile([P, HDIM], U8, align_bytes=64)
        w_grp = const.tile([P, 2, KDIM, 4], BF16, align_bytes=64)
        w_codes = const.tile([P, 2, KDIM], U32, align_bytes=64)
        w_scl = const.tile([P, 2, KDIM], U8, align_bytes=64)

        def regroup(eng, dst, src, factor):
            if eng == "v":
                nc.vector.tensor_copy(out=dst, in_=src)
            elif eng == "s":
                nc.scalar.copy(out=dst, in_=src)
            else:
                nc.gpsimd.tensor_scalar(
                    out=dst, in0=src, scalar1=factor, scalar2=0.0, op0=ALU.mult, op1=ALU.add
                )

        def w_regroup(g, cb, eng):
            cols = slice(cb * HDIM, (cb + 1) * HDIM)
            src = w_raw[:, 4 * g : 4 * g + 4, cols].rearrange("q t c -> q c t")
            regroup(eng, w_grp[:, g, cols, :], src, 1.0)

        def w_quant(g, cb):
            cols = slice(cb * HDIM, (cb + 1) * HDIM)
            nc.vector.quantize_mx(
                out=w_codes[:, g, cols].bitcast(FP8X4),
                scales=w_scl[:, g, cols],
                in_=w_grp[:, g, cols, :].rearrange("q c t -> q (c t)"),
            )

        grps = {}
        codes = {}
        tpt = {}

        pxs = {}

        def perm(c, op):
            words = (xs if op == 0 else hs)[c][:].bitcast(F32).rearrange("p (t w) -> p t w", t=TILES)
            px = quant.tile([P, TILES, 2, P], F32, tag="px%d" % op, bufs=1)
            first = max(op - 1, 0) * 2 * P
            nc.scalar.copy(
                out=px[:], in_=words[:, :, first : first + 2 * P].rearrange("p t (w u) -> p t u w", u=2)
            )
            pxs[(c, op)] = px

        def tr_pe(c, op, hh, bank):
            if op == 0:
                words = xs[c][:].bitcast(F32)
                wpt = XDIM // 2
                g = 0
            else:
                words = hs[c][:].bitcast(F32)
                wpt = KDIM // 2
                g = op - 1
            tp = banks[bank].tile([P, 2, 2 * P], F32, tag=bank)
            for u in range(2):
                for tt in range(2):
                    col = (2 * hh + tt) * wpt + 2 * g * P
                    src = words[:, col + u : col + 2 * P : 2]
                    if (c, op) in pxs:
                        src = pxs[(c, op)][:, 2 * hh + tt, u, :]
                    nc.tensor.transpose(tp[:, u, tt * P : (tt + 1) * P], src, ident[:])
            tpt[(c, op, hh)] = tp

        def tr_cp(c, op, hh, on_vector):
            if hh == 0:
                grp = quant.tile([P, CHUNK * 4], BF16, tag="grp%d" % op, align_bytes=64)
                grps[(c, op)] = grp
            dst = grps[(c, op)][:].bitcast(F32).rearrange("p (n u) -> p n u", u=2)
            dst = dst[:, hh * 2 * P : (hh + 1) * 2 * P, :]
            src = tpt[(c, op, hh)][:].rearrange("p u n -> p n u")
            if on_vector:
                nc.vector.tensor_copy(out=dst, in_=src)
            else:
                nc.scalar.copy(out=dst, in_=src)

        def tr_quant(c, op):
            cd = quant.tile([P, CHUNK], U32, tag="cd%d" % op, align_bytes=64)
            sc = quant.tile([P, CHUNK], U8, tag="sc%d" % op, align_bytes=64)
            nc.vector.quantize_mx(out=cd[:].bitcast(FP8X4), scales=sc[:], in_=grps[(c, op)][:])
            codes[(c, op)] = (cd, sc)

        fzs = {}
        ys = {}
        gts = {}

        def fi_pe(c, jt, bank):
            cd, sc = codes[(c, 0)]
            cols = slice(jt * P, (jt + 1) * P)
            fz = banks[bank].tile([P, CHUNK], F32, tag=bank)
            nc.tensor.matmul_mx(
                out=fz[:],
                lhsT=wf_codes[:, cols].bitcast(FP8X4),
                lhsT_scale=wf_scl[:, cols],
                rhs=cd[:].bitcast(FP8X4),
                rhs_scale=sc[:],
                start=True,
                stop=True,
            )
            fzs[(c, jt)] = fz

        def fi_y(c, jt):
            y2 = work.tile([P, CHUNK], F32, tag="y%d" % jt)
            nc.scalar.activation(
                out=y2[:], in_=fzs[(c, jt)][:], func=AF.Identity, bias=bf2[:, jt : jt + 1], scale=1.0
            )
            ys[(c, jt)] = y2

        def fi_g(c, jt):
            gt = work.tile([P, CHUNK], F32, tag="g%d" % jt)
            nc.gpsimd.tensor_tensor(
                out=gt[:].rearrange("q (t p) -> q t p", t=TILES),
                in0=ys[(c, jt)][:].rearrange("q (t p) -> q t p", t=TILES),
                in1=ms[c].rearrange("q (p t) -> q t p", t=TILES),
                op=ALU.mult,
            )
            gts[(c, jt)] = gt

        def fi_first(jt):
            gt = work.tile([P, CHUNK], F32, tag="g%d" % jt)
            nc.vector.scalar_tensor_tensor(
                out=gt[:].rearrange("q (t p) -> q t p", t=TILES),
                in0=fzs[(0, jt)][:].rearrange("q (t p) -> q t p", t=TILES),
                scalar=bf2[:, jt : jt + 1],
                in1=ms[0].rearrange("q (p t) -> q t p", t=TILES),
                op0=ALU.add,
                op1=ALU.mult,
            )
            gts[(0, jt)] = gt

        zts = {}
        fts = {}

        def z_pe(c, k, jt):
            ct = 2 * k + jt
            cols = slice(ct * P, (ct + 1) * P)
            zp = zps.tile([P, CHUNK], F32, tag="z")
            for g in range(2):
                cd, sc = codes[(c, 1 + g)]
                nc.tensor.matmul_mx(
                    out=zp[:],
                    lhsT=w_codes[:, g, cols].bitcast(FP8X4),
                    lhsT_scale=w_scl[:, g, cols],
                    rhs=cd[:].bitcast(FP8X4),
                    rhs_scale=sc[:],
                    start=(g == 0),
                    stop=(g == 1),
                )
            zts[(c, ct)] = zp

        def gate(c, k, jt):
            ct = 2 * k + jt
            f_sb = work.tile([P, CHUNK], F32, tag="f", bufs=12)
            nc.vector.tensor_tensor(out=f_sb[:], in0=zts[(c, ct)][:], in1=gts[(c, jt)][:], op=ALU.add)
            nc.scalar.activation(
                out=f_sb[:], in_=f_sb[:], func=AF.Sigmoid, bias=bias[:, ct : ct + 1], scale=1.0
            )
            fts[(c, ct)] = f_sb

        fbs = {}
        prods = {}
        accs = {}

        def fb_pe(c, k, hh):
            fb = fps.tile([P, 2, HDIM], F32, tag="fb")
            for tt in range(2):
                t = 2 * hh + tt
                for jt in range(2):
                    nc.tensor.transpose(
                        fb[:, tt, jt * P : (jt + 1) * P],
                        fts[(c, 2 * k + jt)][:, t * P : (t + 1) * P],
                        ident[:],
                    )
            fbs[(c, k, hh)] = fb

        def times_c(c, k, hh):
            if (c, k) not in prods:
                prod = work.tile([P, TILES, HDIM], F32, tag="prod", bufs=8)
                prods[(c, k)] = prod
            half = slice(2 * hh, 2 * hh + 2)
            c4 = cs[c][:].rearrange("p (t k j) -> p t k j", t=TILES, k=KIDS)
            nc.vector.tensor_tensor(
                out=prods[(c, k)][:, half, :], in0=fbs[(c, k, hh)][:], in1=c4[:, half, k, :], op=ALU.mult
            )

        def add(eng, c, k, half):
            acc = accs[c][:, half, :]
            first = prods[(c, 0)][:, half, :] if k == 1 else acc
            eng.tensor_tensor(out=acc, in0=first, in1=prods[(c, k)][:, half, :], op=ALU.add)

        def finish_last(k):
            c = NCHUNK - 1
            halves = (slice(0, 2), slice(2, 4))
            if k == 1:
                add(nc.gpsimd, c, 1, halves[0])
                add(nc.gpsimd, c, 1, halves[1])
            if k == 2:
                add(nc.gpsimd, c, 2, halves[1])
            if k == 3:
                p3 = prods[(c, 3)][:, halves[0], :]
                nc.vector.tensor_tensor(out=p3, in0=p3, in1=prods[(c, 2)][:, halves[0], :], op=ALU.add)
                for hh in range(2):
                    add(nc.vector, c, 3, halves[hh])
                    nc.sync.dma_start(
                        out=o_v[c][:, hh * 2 * HDIM : (hh + 1) * 2 * HDIM],
                        in_=accs[c][:, halves[hh], :].rearrange("p t j -> p (t j)"),
                    )

        def finish(c, k):
            last = c == NCHUNK - 1
            if k == 1:
                acc = work.tile([P, TILES, HDIM], F32, tag="acc")
                accs[c] = acc
            for hh in range(2):
                times_c(c, k, hh)
            if last:
                finish_last(k)
                return
            if k >= 1:
                add(nc.gpsimd, c, k, slice(0, TILES))
            if k == 3:
                nc.sync.dma_start(out=o_v[c], in_=accs[c][:].rearrange("p t j -> p (t j)"))

        idle_in = const.tile([P, CHUNK], BF16)
        nc.vector.memset(idle_in[:].bitcast(U32), 0)

        def spin(n):
            idle_out = fps.tile([P, CHUNK], F32, tag="fb")
            for i in range(n):
                nc.tensor.matmul(idle_out[:], lhsT=idle_in[:, 0:P], rhs=idle_in[:], start=True, stop=True)

        spin(5)
        warm = const.tile([P, 1], F32)
        nc.vector.memset(warm[:], 0.0)
        nc.scalar.activation(out=warm[:], in_=warm[:], func=AF.Sigmoid)
        regroup("g", wf_grp[:], wf_raw[:].rearrange("q t c -> q c t"), 2.0)
        tr_pe(0, 0, 0, "tp")
        tr_pe(0, 0, 1, "tp")
        spin(2)
        tr_cp(0, 0, 0, False)
        tr_cp(0, 0, 1, True)
        tr_quant(0, 0)
        nc.vector.quantize_mx(
            out=wf_codes[:].bitcast(FP8X4),
            scales=wf_scl[:],
            in_=wf_grp[:].rearrange("q c t -> q (c t)"),
        )
        tr_pe(0, 1, 0, "fb")
        tr_pe(0, 2, 0, "fb")
        bias_ps = zps.tile([P, P], BF16, tag="z")
        nc.tensor.transpose(bias_ps[:], bias_rows[:], ident_bf[:])
        m_ps = zps.tile([P, CHUNK], F32, tag="z")
        nc.tensor.matmul(m_ps[:], lhsT=ones[:], rhs=m_row[:], start=True, stop=True)
        tr_pe(0, 1, 1, "z")
        tr_pe(0, 2, 1, "z")
        fi_pe(0, 0, "tp")
        fi_pe(0, 1, "tp")
        spin(2)
        w_regroup(0, 0, "g")
        w_regroup(1, 0, "s")
        w_quant(0, 0)
        w_quant(1, 0)
        tr_cp(0, 1, 0, False)
        tr_cp(0, 2, 0, False)
        nc.scalar.copy(out=m_first[:], in_=m_ps[:])
        nc.vector.tensor_copy(out=bias[:, 0:10], in_=bias_ps[:, 0:10])
        nc.vector.tensor_scalar_mul(out=bf2[:], in0=bias[:, 8:10], scalar1=2.0)
        tr_cp(0, 1, 1, False)
        tr_cp(0, 2, 1, False)
        tr_quant(0, 1)
        tr_quant(0, 2)
        fi_first(0)
        fi_first(1)
        for cb in range(1, 4):
            w_regroup(0, cb, "g")
            w_regroup(1, cb, "s")

        total = NCHUNK * KIDS
        for i in range(total + LAG):
            c, j = divmod(i, KIDS)
            live = i < total
            units = []
            early = []
            quants = []
            if i < KIDS:
                units = [[(1, 0)], [(1, 1)], [(1, 2)], [(2, 0)]][i]
                early = [[], [], [], [(1, 2)]][i]
                quants = [[], [(1, 0)], [(1, 1)], []][i]
            elif live:
                if j < 2 and c + 1 < NCHUNK:
                    units.append((c + 1, j + 1))
                if j == 3 and c + 2 < NCHUNK:
                    units.append((c + 2, 0))
                if j < 3 and c + 1 < NCHUNK:
                    quants.append((c + 1, j))
            fi_now = live and c + 1 < NCHUNK and j == 2
            if live:
                z_pe(c, j, 0)
                z_pe(c, j, 1)
            if fi_now:
                fi_pe(c + 1, 0, "tp")
                fi_pe(c + 1, 1, "tp")
            for cc, op in units:
                tr_pe(cc, op, 0, "tp")
                tr_pe(cc, op, 1, "tp")
            if i >= LAG:
                c2, k2 = divmod(i - LAG, KIDS)
                fb_pe(c2, k2, 0)
                fb_pe(c2, k2, 1)
            if live and j == 0:
                if c + 2 < NCHUNK:
                    load_h(c + 2)
                if c + 3 < NCHUNK:
                    load_x(c + 3)
                if i == 0:
                    load_c(2)
            if live and i >= 3 and j == 2 and c + 2 < NCHUNK:
                perm(c + 2, 0)
            if fi_now:
                for jt in range(2):
                    fi_y(c + 1, jt)
                    fi_g(c + 1, jt)
            for cc, op in units:
                tr_cp(cc, op, 0, False)
                tr_cp(cc, op, 1, False)
            if live:
                gate(c, j, 0)
                if i < 3:
                    w_quant(0, i + 1)
                    w_quant(1, i + 1)
                gate(c, j, 1)
            for cc, op in early:
                tr_quant(cc, op)
            if i >= LAG:
                c2, k2 = divmod(i - LAG, KIDS)
                finish(c2, k2)
                if k2 == 3 and c2 + 3 < NCHUNK:
                    load_c(c2 + 3)
            for cc, op in quants:
                tr_quant(cc, op)
